import numpy as np
import ml_dtypes


def mxq(x, axis, fmt="e4m3"):
    dtype, down = {"e4m3": (ml_dtypes.float8_e4m3fn, 7), "e5m2": (ml_dtypes.float8_e5m2, 14)}[fmt]
    v = np.moveaxis(np.asarray(x, np.float32).astype(ml_dtypes.bfloat16).astype(np.float64), axis, -1)
    blocks = v.reshape(v.shape[:-1] + (-1, 32))
    amax = np.abs(blocks).max(-1, keepdims=True)
    byte = np.maximum(np.where(amax > 0, np.frexp(amax)[1] - 1 + 127, 0) - down, 1)
    scale = np.exp2(byte - 127.0)
    codes = (blocks / scale).astype(np.float32).astype(dtype).astype(np.float64)
    return np.moveaxis((codes * scale).reshape(v.shape), -1, axis)


WIDE = False


def mx_kscale(k):
    if not WIDE:
        return np.ones(k)
    levels = np.array([10, -10, 5, -5, 0])
    if k % 512:
        return np.exp2(np.random.permutation(np.resize(levels, k // 32))).repeat(32)
    a = np.empty((k // 512, 16))
    for p in range(k // 512):
        a[p, :8] = np.random.permutation(np.resize(levels, 8))
        for g in range(8):
            far = levels[np.abs(levels - a[p, g]) >= 10]
            a[p, g + 8] = far[np.random.randint(len(far))]
    return np.exp2(a.ravel()).repeat(32)


BF16 = ml_dtypes.bfloat16


def bf(x):
    return np.asarray(x, np.float32).astype(BF16)


def f64(x):
    return np.asarray(x).astype(np.float64)


B, S, E, H, KVH, D = 1, 512, 2048, 16, 4, 128
ROPE_THETA = 10000.0


def rope(t):
    inv_freq = 1.0 / ROPE_THETA ** (np.arange(0, D, 2) / D)
    freqs = np.arange(S)[:, None] * inv_freq[None, :]
    cos = np.concatenate([np.cos(freqs), np.cos(freqs)], axis=-1)
    sin = np.concatenate([np.sin(freqs), np.sin(freqs)], axis=-1)
    t1, t2 = np.split(t, 2, axis=-1)
    rotated = np.concatenate([-t2, t1], axis=-1)
    return t * cos + rotated * sin


def draw0():
    s = mx_kscale(E)
    return {"x": bf(np.random.standard_normal((B, S, E)) * s),
            "Wq": bf(np.random.standard_normal((H * D, E)) * 1.3 / np.sqrt(E) / s),
            "bq": bf(np.random.standard_normal(H * D) * 0.5),
            "Wkv": bf(np.random.standard_normal((2 * KVH * D, E)) * 1.3 / np.sqrt(E) / s),
            "bkv": bf(np.random.standard_normal(2 * KVH * D) * 0.5)}


def core(x, Wq, bq, Wkv, bkv):
    xq = mxq(f64(x), 2, "e4m3")
    q = (xq @ mxq(f64(Wq), 1, "e4m3").T) + f64(bq)
    kv = (xq @ mxq(f64(Wkv), 1, "e4m3").T) + f64(bkv)
    k, v = np.split(kv, 2, axis=-1)
    q = q.reshape(B, S, H, D).transpose(0, 2, 1, 3)
    k = k.reshape(B, S, KVH, D).transpose(0, 2, 1, 3)
    v = v.reshape(B, S, KVH, D).transpose(0, 2, 1, 3)
    return rope(q), rope(k), v


def e4m3fn_bytes(y):
    return np.clip(np.asarray(y, np.float64), -448.0, 448.0).astype(np.float32).astype(ml_dtypes.float8_e4m3fn).view(np.uint8)


def e4m3fn_values(b):
    return np.asarray(b, np.uint8).view(ml_dtypes.float8_e4m3fn).astype(np.float64)


def setup_inputs():
    d = draw0()
    x0 = np.asarray(d['Wq']).astype(np.float64)
    s = (np.max(np.abs(x0), axis=(0,), keepdims=True) / 448.0).astype(np.float32)
    out = {}
    for k, v in d.items():
        if k == 'Wq':
            out['Wq_bytes'] = e4m3fn_bytes(x0 / s.astype(np.float64))
            out['Wq_scale'] = s
        else:
            out[k] = v
    return out


def reference(x, Wq_bytes, Wq_scale, bq, Wkv, bkv):
    return core(x, e4m3fn_values(Wq_bytes) * Wq_scale.astype(np.float64), bq, Wkv, bkv)

@@ -1,0 +1,349 @@
+from contextlib import ExitStack
+import math
+
+import concourse.mybir as mybir
+from concourse.masks import make_identity
+
+FLOPS = 2 * 512 * 2048 * 3072
+
+F32 = mybir.dt.float32
+BF16 = mybir.dt.bfloat16
+I32 = mybir.dt.int32
+U32 = mybir.dt.uint32
+U8 = mybir.dt.uint8
+FP8 = mybir.dt.float8_e4m3fn
+FP8X4 = mybir.dt.float8_e4m3fn_x4
+ALU = mybir.AluOpType
+ACT = mybir.ActivationFunctionType
+
+P = 128
+E = 2048
+PASSES = 4
+TT = 4
+HALF = 64
+ROPE_THETA = 10000.0
+TWO_PI = 2.0 * math.pi
+TWO_PI_HEAD = 6.28125
+TWO_PI_TAIL = TWO_PI - TWO_PI_HEAD
+PI_BELOW = 3.1415925
+
+
+def tile_qwen2attention_pa_kernel(tc, x, Wq_bytes, Wq_scale, bq, Wkv, bkv, out_0, out_1, out_2):
+    nc = tc.nc
+
+    order = []
+    for i in range(8):
+        order.append(("q", 2 * i))
+        order.append(("q", 2 * i + 1))
+        order.append(("v", i) if i < 4 else ("k", i - 4))
+    n_tiles = len(order)
+
+    with ExitStack() as ctx:
+        const = ctx.enter_context(tc.tile_pool(name="const", bufs=1))
+        work = ctx.enter_context(tc.tile_pool(name="work", bufs=3))
+        psum = ctx.enter_context(tc.psum_pool(name="psum", bufs=2))
+        ctx.enter_context(tc.manual_schedule())
+
+        scale_rows = const.tile([P, P], F32, name="scale_rows")
+        nc.gpsimd.memset(scale_rows[:], 0.0)
+        bias_rows = const.tile([P, P], BF16, name="bias_rows")
+        nc.gpsimd.memset(bias_rows[:], 0.0)
+        warm = const.tile([P, 2], F32, name="warm")
+        nc.gpsimd.memset(warm[:, 0:1], 0.0)
+        pos_i = const.tile([P, TT], I32, name="pos_i")
+        nc.gpsimd.iota(pos_i[:], pattern=[[1, TT]], base=0, channel_multiplier=TT)
+        ident = const.tile([P, P], F32, name="ident")
+        make_identity(nc, ident[:])
+
+        nc.sync.dma_start(out=scale_rows[0:16, :], in_=Wq_scale.rearrange("o (c p) -> (o c) p", p=P))
+        nc.sync.dma_start(out=bias_rows[0:16, :], in_=bq.rearrange("(c p) -> c p", p=P))
+        nc.sync.dma_start(out=bias_rows[16:24, :], in_=bkv.rearrange("(c p) -> c p", p=P))
+        bias_f32 = const.tile([P, P], F32, name="bias_f32")
+        nc.gpsimd.tensor_copy(out=bias_f32[:], in_=bias_rows[:])
+
+        wq_view = Wq_bytes.rearrange("(m p) k -> p m k", p=P)
+        wq_bytes = {}
+        wkv_raw = {}
+        x_raw = []
+
+        def load_wq(pair):
+            t = const.tile([P, 2, E], U8, name="wq_bytes%d" % pair)
+            nc.sync.dma_start(out=t[:], in_=wq_view[:, 2 * pair : 2 * pair + 2, :])
+            wq_bytes[pair] = t
+
+        def load_wkv(m):
+            t = const.tile([P, E], BF16, name="wkv_raw%d" % m)
+            nc.sync.dma_start(out=t[:], in_=Wkv[m * P : (m + 1) * P, :])
+            wkv_raw[m] = t
+
+        load_wq(0)
+        x_view = x.rearrange("o (p t) k -> (o t) p k", t=TT)
+        for tt in range(TT):
+            t = const.tile([P, E], BF16, name="x_raw%d" % tt)
+            nc.sync.dma_start(out=t[:], in_=x_view[tt])
+            x_raw.append(t)
+        load_wq(1)
+        for kind, h in order:
+            if kind == "q":
+                if h // 2 not in wq_bytes:
+                    load_wq(h // 2)
+            else:
+                load_wkv(h if kind == "k" else 4 + h)
+
+        nc.scalar.activation(out=warm[:, 1:2], in_=warm[:, 0:1], func=ACT.Sin)
+        pos = const.tile([P, TT], F32, name="pos")
+        nc.vector.tensor_copy(out=pos[:], in_=pos_i[:])
+        freq = const.tile([P, HALF], F32, name="freq")
+        nc.vector.memset(freq[:, 0:1], 1.0)
+        for b in range(6):
+            n = 1 << b
+            nc.vector.tensor_scalar(
+                out=freq[:, n : 2 * n], in0=freq[:, 0:n], scalar1=ROPE_THETA ** (-n / 64.0), scalar2=None, op0=ALU.mult
+            )
+        ang = const.tile([P, TT * HALF], F32, name="ang")
+        for tt in range(TT):
+            nc.vector.tensor_scalar(
+                out=ang[:, tt * HALF : (tt + 1) * HALF], in0=freq[:], scalar1=pos[:, tt : tt + 1], scalar2=None, op0=ALU.mult
+            )
+        turns_i = const.tile([P, 256], I32, name="turns_i")
+        nc.vector.tensor_scalar(out=turns_i[:], in0=ang[:], scalar1=1.0 / TWO_PI, scalar2=None, op0=ALU.mult)
+        turns = const.tile([P, 256], F32, name="turns")
+        nc.vector.tensor_copy(out=turns[:], in_=turns_i[:])
+        red_a = const.tile([P, 256], F32, name="red_a")
+        nc.vector.scalar_tensor_tensor(out=red_a[:], in0=turns[:], scalar=-TWO_PI_HEAD, in1=ang[:], op0=ALU.mult, op1=ALU.add)
+        red_b = const.tile([P, 256], F32, name="red_b")
+        nc.vector.scalar_tensor_tensor(out=red_b[:], in0=turns[:], scalar=-TWO_PI_TAIL, in1=red_a[:], op0=ALU.mult, op1=ALU.add)
+        wrap = const.tile([P, 256], F32, name="wrap")
+        nc.vector.tensor_scalar(out=wrap[:], in0=red_b[:], scalar1=math.pi, scalar2=-TWO_PI, op0=ALU.is_gt, op1=ALU.mult)
+        red_c = const.tile([P, 256], F32, name="red_c")
+        nc.vector.tensor_tensor(out=red_c[:], in0=red_b[:], in1=wrap[:], op=ALU.add)
+        red_d = const.tile([P, 256], F32, name="red_d")
+        nc.vector.tensor_scalar(out=red_d[:], in0=red_c[:], scalar1=PI_BELOW, scalar2=-PI_BELOW, op0=ALU.min, op1=ALU.max)
+
+        scale_bank = psum.tile([P, P], F32, tag="fwd", bufs=4, name="scale_bank")
+        nc.tensor.transpose(scale_bank[:], scale_rows[:], ident[:])
+        scale_col = const.tile([P, 16], F32, name="scale_col")
+        nc.scalar.copy(out=scale_col[:], in_=scale_bank[:, 0:16])
+        scale_all = [const.tile([P, 1024], F32, name="scale_all%d" % part) for part in range(2)]
+        for b in range(4):
+            bank = psum.tile([P, 4, P], F32, tag="fwd", bufs=4, name="spread_bank")
+            for c in range(4):
+                nc.tensor.transpose(bank[:, c, :], scale_col[:, 4 * b + c : 4 * b + c + 1].to_broadcast([P, P]), ident[:])
+            dst = scale_all[b // 2][:, (b % 2) * 512 : (b % 2 + 1) * 512]
+            if b % 2 == 0:
+                nc.scalar.copy(out=dst, in_=bank[:].rearrange("p c k -> p (c k)"))
+            else:
+                nc.vector.tensor_copy(out=dst, in_=bank[:].rearrange("p c k -> p (c k)"))
+
+        def turn(src, out_views, sorted_words=None):
+            words = src.bitcast(F32)
+            for gp in range(2):
+                bank = psum.tile([P, 2, 2, P], F32, tag="fwd", bufs=4, name="fwd_bank")
+                for gi in range(2):
+                    g = 2 * gp + gi
+                    for u in range(2):
+                        if sorted_words is None:
+                            picked = words[:, 256 * g + u : 256 * (g + 1) : 2]
+                        else:
+                            picked = sorted_words[:, (2 * g + u) * P : (2 * g + u + 1) * P]
+                        nc.tensor.transpose(bank[:, gi, u, :], picked, ident[:])
+                nc.scalar.copy(out=out_views[gp], in_=bank[:].rearrange("p g u r -> p g r u"))
+
+        sorted_of = {}
+
+        def sort_words(i):
+            if i >= n_tiles or i % 3 == 0:
+                return
+            sw = work.tile([P, 1024], F32, tag="sw", bufs=3, name="sw")
+            nc.scalar.copy(
+                out=sw[:].rearrange("p (g u w) -> p g u w", g=PASSES, u=2),
+                in_=src_of[i][:].bitcast(F32).rearrange("p (g w u) -> p g u w", g=PASSES, u=2),
+            )
+            sorted_of[i] = sw
+
+        src_of = {}
+        grp_of = {}
+        codes_of = {}
+        acc_of = {}
+        uw_of = {}
+
+        def product(i, part):
+            if i >= n_tiles:
+                return
+            kind, h = order[i]
+            if kind == "q":
+                if part == 0:
+                    src_of[i] = work.tile([P, E], BF16, tag="wbf", bufs=6, name="wbf")
+                cols = slice(part * 1024, (part + 1) * 1024)
+                nc.vector.tensor_tensor(
+                    out=src_of[i][:, cols],
+                    in0=wq_bytes[h // 2][:, h % 2, cols].bitcast(FP8),
+                    in1=scale_all[part][:],
+                    op=ALU.mult,
+                )
+            elif kind == "k":
+                src_of[i] = wkv_raw[h]
+            else:
+                src_of[i] = wkv_raw[4 + h]
+
+        def turn_w(i):
+            if i >= n_tiles:
+                return
+            grp = work.tile([P, E], BF16, tag="grp", bufs=4, align_bytes=64, name="grp")
+            views = [
+                grp[:, gp * 1024 : (gp + 1) * 1024].bitcast(F32).rearrange("p (g r u) -> p g r u", g=2, u=2)
+                for gp in range(2)
+            ]
+            turn(src_of[i][:], views, sorted_of.get(i))
+            grp_of[i] = grp
+
+        def quant(i):
+            if i >= n_tiles:
+                return
+            wc = work.tile([P, 512], U32, tag="wc", bufs=3, align_bytes=64, name="wc")
+            ws = work.tile([P, 512], U8, tag="ws", bufs=3, align_bytes=64, name="ws")
+            nc.vector.quantize_mx(out=wc[:].bitcast(FP8X4), scales=ws[:], in_=grp_of[i][:])
+            codes_of[i] = (wc, ws)
+
+        def mx(i):
+            if i >= n_tiles:
+                return
+            wc, ws = codes_of[i]
+            acc = psum.tile([P, 512], F32, tag="acc", bufs=2, name="acc")
+            for g in range(PASSES):
+                cols = slice(g * P, (g + 1) * P)
+                nc.tensor.matmul_mx(
+                    out=acc[:],
+                    lhsT=wc[:, cols].bitcast(FP8X4),
+                    lhsT_scale=ws[:, cols],
+                    rhs=x_codes[g][:].bitcast(FP8X4),
+                    rhs_scale=x_scales[g][:],
+                    start=(g == 0),
+                    stop=(g == PASSES - 1),
+                )
+            acc_of[i] = acc
+
+        def bias_col(i):
+            kind, h = order[i]
+            m = h if kind == "q" else (16 + h if kind == "k" else 20 + h)
+            return bias_ch[:, m : m + 1]
+
+        def rope(i):
+            if i < 0 or i >= n_tiles:
+                return
+            kind, h = order[i]
+            acc = acc_of[i]
+            uw = work.tile([P, 2, 512], F32, tag="uw", bufs=3, name="uw")
+            if kind == "v":
+                nc.scalar.activation(out=uw[:, 0, :], in_=acc[:], func=ACT.Identity, bias=bias_col(i), scale=1.0)
+            else:
+                nc.vector.scalar_tensor_tensor(
+                    out=uw[:],
+                    in0=acc[:].unsqueeze(1).to_broadcast([P, 2, 512]),
+                    scalar=bias_col(i),
+                    in1=cs_ch[:],
+                    op0=ALU.add,
+                    op1=ALU.mult,
+                )
+            uw_of[i] = uw
+
+        out_views = {
+            "q": out_0.rearrange("o h (p t) d -> (o h) p (t d)", t=TT),
+            "k": out_1.rearrange("o h (p t) d -> (o h) p (t d)", t=TT),
+            "v": out_2.rearrange("o h (p t) d -> (o h) p (t d)", t=TT),
+        }
+
+        def back(i):
+            if i < 0 or i >= n_tiles:
+                return
+            kind, h = order[i]
+            uw = uw_of[i]
+            po = psum.tile([P, TT, P], F32, tag="back", bufs=2, name="po")
+            for tt in range(TT):
+                cols = slice(tt * P, (tt + 1) * P)
+                if kind == "v":
+                    nc.tensor.transpose(po[:, tt, :], uw[:, 0, cols], ident[:])
+                else:
+                    nc.tensor.matmul(
+                        out=po[:, tt, :], lhsT=uw[:, 0, cols], rhs=ident[:], start=True, stop=False, is_transpose=True
+                    )
+                    nc.tensor.matmul(
+                        out=po[:, tt, :], lhsT=uw[:, 1, cols], rhs=swap[:], start=False, stop=True, is_transpose=True
+                    )
+            o = work.tile([P, 512], F32, tag="o", bufs=3, name="o")
+            nc.scalar.copy(out=o[:], in_=po[:].rearrange("p t d -> p (t d)"))
+            nc.sync.dma_start(out=out_views[kind][h], in_=o[:])
+
+        x_grp = [const.tile([P, 2 * TT * P * 4], BF16, align_bytes=64, name="x_grp%d" % gp) for gp in range(2)]
+
+        def turn_x(tt):
+            views = [
+                x_grp[gp][:].bitcast(F32).rearrange("p (g t r u) -> p g t r u", g=2, t=TT, u=2)[:, :, tt, :, :]
+                for gp in range(2)
+            ]
+            turn(x_raw[tt][:], views)
+
+        product(0, 0)
+        product(0, 1)
+        turn_x(0)
+        turn_x(1)
+        product(1, 0)
+        product(1, 1)
+        turn_x(2)
+        turn_x(3)
+        turn_w(0)
+        product(2, 0)
+        product(3, 0)
+        x_codes = []
+        x_scales = []
+        for g in range(PASSES):
+            xc = const.tile([P, 512], U32, align_bytes=64, name="x_codes%d" % g)
+            xs = const.tile([P, 512], U8, align_bytes=64, name="x_scales%d" % g)
+            nc.vector.quantize_mx(
+                out=xc[:].bitcast(FP8X4), scales=xs[:], in_=x_grp[g // 2][:, (g % 2) * 2048 : (g % 2 + 1) * 2048]
+            )
+            x_codes.append(xc)
+            x_scales.append(xs)
+        quant(0)
+        turn_w(1)
+        mx(0)
+        product(3, 1)
+
+        y_sin = red_d[:].rearrange("p (t j) -> p t j", j=HALF)
+        y_abs = const.tile([P, TT, HALF], F32, name="y_abs")
+        nc.scalar.activation(out=y_abs[:], in_=y_sin, func=ACT.Abs)
+        cos_tok = const.tile([P, TT, P], F32, name="cos_tok")
+        sin_tok = const.tile([P, TT, P], F32, name="sin_tok")
+        nc.scalar.activation(out=sin_tok[:, :, 0:HALF], in_=y_sin, func=ACT.Sin)
+        nc.scalar.activation(out=sin_tok[:, :, HALF:P], in_=y_sin, func=ACT.Sin, scale=-1.0)
+        nc.scalar.activation(out=cos_tok[:, :, 0:HALF], in_=y_abs[:], func=ACT.Sin, scale=-1.0, bias=math.pi / 2.0)
+        nc.scalar.activation(out=cos_tok[:, :, HALF:P], in_=y_abs[:], func=ACT.Sin, scale=-1.0, bias=math.pi / 2.0)
+        cs_ch = const.tile([P, 2, 512], F32, name="cs_ch")
+        for which, src_t in enumerate((cos_tok, sin_tok)):
+            bank = psum.tile([P, TT, P], F32, tag="fwd", bufs=4, name="table_bank")
+            for tt in range(TT):
+                nc.tensor.transpose(bank[:, tt, :], src_t[:, tt, :], ident[:])
+            nc.scalar.copy(out=cs_ch[:, which, :], in_=bank[:].rearrange("p t s -> p (t s)"))
+        bias_bank = psum.tile([P, P], F32, tag="fwd", bufs=4, name="bias_bank")
+        nc.tensor.transpose(bias_bank[:], bias_f32[:], ident[:])
+        bias_ch = const.tile([P, 24], F32, name="bias_ch")
+        nc.scalar.copy(out=bias_ch[:], in_=bias_bank[:, 0:24])
+        swap = const.tile([P, P], F32, name="swap")
+        nc.vector.tensor_copy(out=swap[:, 0:HALF], in_=ident[:, HALF:P])
+        nc.vector.tensor_copy(out=swap[:, HALF:P], in_=ident[:, 0:HALF])
+
+        product(4, 0)
+        product(4, 1)
+        turn_w(2)
+        sort_words(4)
+        product(5, 0)
+
+        for step in range(1, n_tiles + 2):
+            quant(step)
+            product(step + 5, 0)
+            rope(step - 1)
+            product(step + 5, 1)
+            back(step - 2)
+            turn_w(step + 2)
+            sort_words(step + 4)
+            mx(step)

@@ -205,12 +205,14 @@ def tile_qwen2attention_pa_kernel(tc, x, Wq_bytes, Wq_scale, bq, Wkv, bkv, out_0
             nc.vector.quantize_mx(out=wc[:].bitcast(FP8X4), scales=ws[:], in_=grp_of[i][:])
             codes_of[i] = (wc, ws)
 
-        def mx(i):
+        def mx(i, first, last):
             if i >= n_tiles:
                 return
             wc, ws = codes_of[i]
-            acc = psum.tile([P, 512], F32, tag="acc", bufs=2, name="acc")
-            for g in range(PASSES):
+            if first == 0:
+                acc_of[i] = psum.tile([P, 512], F32, tag="acc", bufs=2, name="acc")
+            acc = acc_of[i]
+            for g in range(first, last):
                 cols = slice(g * P, (g + 1) * P)
                 nc.tensor.matmul_mx(
                     out=acc[:],
@@ -221,7 +223,6 @@ def tile_qwen2attention_pa_kernel(tc, x, Wq_bytes, Wq_scale, bq, Wkv, bkv, out_0
                     start=(g == 0),
                     stop=(g == PASSES - 1),
                 )
-            acc_of[i] = acc
 
         def bias_col(i):
             kind, h = order[i]
@@ -306,7 +307,7 @@ def tile_qwen2attention_pa_kernel(tc, x, Wq_bytes, Wq_scale, bq, Wkv, bkv, out_0
             x_scales.append(xs)
         quant(0)
         turn_w(1)
-        mx(0)
+        mx(0, 0, PASSES)
         product(3, 1)
 
         y_sin = red_d[:].rearrange("p (t j) -> p t j", j=HALF)
@@ -334,16 +335,18 @@ def tile_qwen2attention_pa_kernel(tc, x, Wq_bytes, Wq_scale, bq, Wkv, bkv, out_0
 
         product(4, 0)
         product(4, 1)
+        quant(1)
         turn_w(2)
         sort_words(4)
         product(5, 0)
 
         for step in range(1, n_tiles + 2):
-            quant(step)
             product(step + 5, 0)
             rope(step - 1)
+            quant(step + 1)
             product(step + 5, 1)
             back(step - 2)
+            mx(step, 0, 2)
             turn_w(step + 2)
             sort_words(step + 4)
-            mx(step)
+            mx(step, 2, PASSES)

@@ -33,9 +33,9 @@ def tile_qwen2attention_pa_kernel(tc, x, Wq_bytes, Wq_scale, bq, Wkv, bkv, out_0
 
     order = []
     for i in range(8):
+        order.append(("v", i) if i < 4 else ("k", i - 4))
         order.append(("q", 2 * i))
         order.append(("q", 2 * i + 1))
-        order.append(("v", i) if i < 4 else ("k", i - 4))
     n_tiles = len(order)
 
     with ExitStack() as ctx:
@@ -82,7 +82,6 @@ def tile_qwen2attention_pa_kernel(tc, x, Wq_bytes, Wq_scale, bq, Wkv, bkv, out_0
             t = const.tile([P, E], BF16, name="x_raw%d" % tt)
             nc.sync.dma_start(out=t[:], in_=x_view[tt])
             x_raw.append(t)
-        load_wq(1)
         for kind, h in order:
             if kind == "q":
                 if h // 2 not in wq_bytes:
@@ -152,7 +151,7 @@ def tile_qwen2attention_pa_kernel(tc, x, Wq_bytes, Wq_scale, bq, Wkv, bkv, out_0
         sorted_of = {}
 
         def sort_words(i):
-            if i >= n_tiles or i % 3 == 0:
+            if i >= n_tiles or i % 3 == 1:
                 return
             sw = work.tile([P, 1024], F32, tag="sw", bufs=3, name="sw")
             nc.scalar.copy(
@@ -284,17 +283,17 @@ def tile_qwen2attention_pa_kernel(tc, x, Wq_bytes, Wq_scale, bq, Wkv, bkv, out_0
             ]
             turn(x_raw[tt][:], views)
 
-        product(0, 0)
-        product(0, 1)
-        turn_x(0)
-        turn_x(1)
+        for i in range(0, n_tiles, 3):
+            product(i, 0)
         product(1, 0)
         product(1, 1)
+        turn_x(0)
+        turn_x(1)
+        product(2, 0)
+        product(2, 1)
         turn_x(2)
         turn_x(3)
         turn_w(0)
-        product(2, 0)
-        product(3, 0)
         x_codes = []
         x_scales = []
         for g in range(PASSES):
@@ -307,8 +306,6 @@ def tile_qwen2attention_pa_kernel(tc, x, Wq_bytes, Wq_scale, bq, Wkv, bkv, out_0
             x_scales.append(xs)
         quant(0)
         turn_w(1)
-        mx(0, 0, PASSES)
-        product(3, 1)
 
         y_sin = red_d[:].rearrange("p (t j) -> p t j", j=HALF)
         y_abs = const.tile([P, TT, HALF], F32, name="y_abs")
@@ -333,18 +330,23 @@ def tile_qwen2attention_pa_kernel(tc, x, Wq_bytes, Wq_scale, bq, Wkv, bkv, out_0
         nc.vector.tensor_copy(out=swap[:, 0:HALF], in_=ident[:, HALF:P])
         nc.vector.tensor_copy(out=swap[:, HALF:P], in_=ident[:, 0:HALF])
 
-        product(4, 0)
-        product(4, 1)
-        quant(1)
         turn_w(2)
-        sort_words(4)
+        mx(0, 0, PASSES)
+        quant(1)
         product(5, 0)
+        product(5, 1)
 
         for step in range(1, n_tiles + 2):
-            product(step + 5, 0)
+            if step % 3 == 1:
+                product(step + 3, 0)
+            elif step % 3 == 2:
+                product(step + 6, 0)
+            else:
+                product(step + 5, 1)
             rope(step - 1)
             quant(step + 1)
-            product(step + 5, 1)
+            if step % 3 == 1:
+                product(step + 3, 1)
             back(step - 2)
             mx(step, 0, 2)
             turn_w(step + 2)

@@ -54,6 +54,9 @@ def tile_qwen2attention_pa_kernel(tc, x, Wq_bytes, Wq_scale, bq, Wkv, bkv, out_0
         nc.gpsimd.iota(pos_i[:], pattern=[[1, TT]], base=0, channel_multiplier=TT)
         ident = const.tile([P, P], F32, name="ident")
         make_identity(nc, ident[:])
+        swap = const.tile([P, P], F32, name="swap")
+        nc.gpsimd.tensor_copy(out=swap[:, 0:HALF], in_=ident[:, HALF:P])
+        nc.gpsimd.tensor_copy(out=swap[:, HALF:P], in_=ident[:, 0:HALF])
 
         nc.sync.dma_start(out=scale_rows[0:16, :], in_=Wq_scale.rearrange("o (c p) -> (o c) p", p=P))
         nc.sync.dma_start(out=bias_rows[0:16, :], in_=bq.rearrange("(c p) -> c p", p=P))
@@ -124,7 +127,8 @@ def tile_qwen2attention_pa_kernel(tc, x, Wq_bytes, Wq_scale, bq, Wkv, bkv, out_0
         scale_col = const.tile([P, 16], F32, name="scale_col")
         nc.scalar.copy(out=scale_col[:], in_=scale_bank[:, 0:16])
         scale_all = [const.tile([P, 1024], F32, name="scale_all%d" % part) for part in range(2)]
-        for b in range(4):
+
+        def spread(b):
             bank = psum.tile([P, 4, P], F32, tag="fwd", bufs=4, name="spread_bank")
             for c in range(4):
                 nc.tensor.transpose(bank[:, c, :], scale_col[:, 4 * b + c : 4 * b + c + 1].to_broadcast([P, P]), ident[:])
@@ -151,7 +155,7 @@ def tile_qwen2attention_pa_kernel(tc, x, Wq_bytes, Wq_scale, bq, Wkv, bkv, out_0
         sorted_of = {}
 
         def sort_words(i):
-            if i >= n_tiles or i % 3 == 1:
+            if i >= n_tiles or i % 3 != 0:
                 return
             sw = work.tile([P, 1024], F32, tag="sw", bufs=3, name="sw")
             nc.scalar.copy(
@@ -228,6 +232,9 @@ def tile_qwen2attention_pa_kernel(tc, x, Wq_bytes, Wq_scale, bq, Wkv, bkv, out_0
             m = h if kind == "q" else (16 + h if kind == "k" else 20 + h)
             return bias_ch[:, m : m + 1]
 
+        def pieces_of(i):
+            return 2 if i == n_tiles - 1 else 1
+
         def rope(i):
             if i < 0 or i >= n_tiles:
                 return
@@ -237,14 +244,17 @@ def tile_qwen2attention_pa_kernel(tc, x, Wq_bytes, Wq_scale, bq, Wkv, bkv, out_0
             if kind == "v":
                 nc.scalar.activation(out=uw[:, 0, :], in_=acc[:], func=ACT.Identity, bias=bias_col(i), scale=1.0)
             else:
-                nc.vector.scalar_tensor_tensor(
-                    out=uw[:],
-                    in0=acc[:].unsqueeze(1).to_broadcast([P, 2, 512]),
-                    scalar=bias_col(i),
-                    in1=cs_ch[:],
-                    op0=ALU.add,
-                    op1=ALU.mult,
-                )
+                width = 512 // pieces_of(i)
+                for piece in range(pieces_of(i)):
+                    cols = slice(piece * width, (piece + 1) * width)
+                    nc.vector.scalar_tensor_tensor(
+                        out=uw[:, :, cols],
+                        in0=acc[:, cols].unsqueeze(1).to_broadcast([P, 2, width]),
+                        scalar=bias_col(i),
+                        in1=cs_ch[:, :, cols],
+                        op0=ALU.add,
+                        op1=ALU.mult,
+                    )
             uw_of[i] = uw
 
         out_views = {
@@ -258,21 +268,25 @@ def tile_qwen2attention_pa_kernel(tc, x, Wq_bytes, Wq_scale, bq, Wkv, bkv, out_0
                 return
             kind, h = order[i]
             uw = uw_of[i]
-            po = psum.tile([P, TT, P], F32, tag="back", bufs=2, name="po")
-            for tt in range(TT):
-                cols = slice(tt * P, (tt + 1) * P)
-                if kind == "v":
-                    nc.tensor.transpose(po[:, tt, :], uw[:, 0, cols], ident[:])
-                else:
-                    nc.tensor.matmul(
-                        out=po[:, tt, :], lhsT=uw[:, 0, cols], rhs=ident[:], start=True, stop=False, is_transpose=True
-                    )
-                    nc.tensor.matmul(
-                        out=po[:, tt, :], lhsT=uw[:, 1, cols], rhs=swap[:], start=False, stop=True, is_transpose=True
-                    )
             o = work.tile([P, 512], F32, tag="o", bufs=3, name="o")
-            nc.scalar.copy(out=o[:], in_=po[:].rearrange("p t d -> p (t d)"))
-            nc.sync.dma_start(out=out_views[kind][h], in_=o[:])
+            blocks = TT // pieces_of(i)
+            for piece in range(pieces_of(i)):
+                po = psum.tile([P, blocks, P], F32, tag="back", bufs=2, name="po")
+                for b in range(blocks):
+                    tt = piece * blocks + b
+                    cols = slice(tt * P, (tt + 1) * P)
+                    if kind == "v":
+                        nc.tensor.transpose(po[:, b, :], uw[:, 0, cols], ident[:])
+                    else:
+                        nc.tensor.matmul(
+                            out=po[:, b, :], lhsT=uw[:, 0, cols], rhs=ident[:], start=True, stop=False, is_transpose=True
+                        )
+                        nc.tensor.matmul(
+                            out=po[:, b, :], lhsT=uw[:, 1, cols], rhs=swap[:], start=False, stop=True, is_transpose=True
+                        )
+                part = slice(piece * blocks * P, (piece + 1) * blocks * P)
+                nc.scalar.copy(out=o[:, part], in_=po[:].rearrange("p t d -> p (t d)"))
+                nc.sync.dma_start(out=out_views[kind][h][:, part], in_=o[:, part])
 
         x_grp = [const.tile([P, 2 * TT * P * 4], BF16, align_bytes=64, name="x_grp%d" % gp) for gp in range(2)]
 
@@ -285,7 +299,11 @@ def tile_qwen2attention_pa_kernel(tc, x, Wq_bytes, Wq_scale, bq, Wkv, bkv, out_0
 
         for i in range(0, n_tiles, 3):
             product(i, 0)
+        spread(0)
+        spread(1)
         product(1, 0)
+        spread(2)
+        spread(3)
         product(1, 1)
         turn_x(0)
         turn_x(1)
@@ -326,9 +344,6 @@ def tile_qwen2attention_pa_kernel(tc, x, Wq_bytes, Wq_scale, bq, Wkv, bkv, out_0
         nc.tensor.transpose(bias_bank[:], bias_f32[:], ident[:])
         bias_ch = const.tile([P, 24], F32, name="bias_ch")
         nc.scalar.copy(out=bias_ch[:], in_=bias_bank[:, 0:24])
-        swap = const.tile([P, P], F32, name="swap")
-        nc.vector.tensor_copy(out=swap[:, 0:HALF], in_=ident[:, HALF:P])
-        nc.vector.tensor_copy(out=swap[:, HALF:P], in_=ident[:, 0:HALF])
 
         turn_w(2)
         mx(0, 0, PASSES)

@@ -80,12 +80,16 @@ def tile_qwen2attention_pa_kernel(tc, x, Wq_bytes, Wq_scale, bq, Wkv, bkv, out_0
             wkv_raw[m] = t
 
         load_wq(0)
-        x_view = x.rearrange("o (p t) k -> (o t) p k", t=TT)
-        for tt in range(TT):
-            t = const.tile([P, E], BF16, name="x_raw%d" % tt)
-            nc.sync.dma_start(out=t[:], in_=x_view[tt])
+        scale_kp = const.tile([P, PASSES, 4], F32, name="scale_kp")
+        x_view = x.rearrange("o (p t) k -> p (o t) k", t=TT)
+        for g in range(PASSES):
+            t = const.tile([P, TT, 512], BF16, name="x_raw%d" % g)
+            nc.sync.dma_start(out=t[:], in_=x_view[:, :, g * 512 : (g + 1) * 512])
             x_raw.append(t)
-        for kind, h in order:
+            if g == 1:
+                load_wkv(4)
+        nc.sync.dma_start(out=scale_kp[:], in_=Wq_scale.rearrange("o (g p t) -> p (o g) t", p=P, t=4))
+        for kind, h in order[1:]:
             if kind == "q":
                 if h // 2 not in wq_bytes:
                     load_wq(h // 2)
@@ -133,36 +137,21 @@ def tile_qwen2attention_pa_kernel(tc, x, Wq_bytes, Wq_scale, bq, Wkv, bkv, out_0
             for c in range(4):
                 nc.tensor.transpose(bank[:, c, :], scale_col[:, 4 * b + c : 4 * b + c + 1].to_broadcast([P, P]), ident[:])
             dst = scale_all[b // 2][:, (b % 2) * 512 : (b % 2 + 1) * 512]
-            if b % 2 == 0:
-                nc.scalar.copy(out=dst, in_=bank[:].rearrange("p c k -> p (c k)"))
-            else:
-                nc.vector.tensor_copy(out=dst, in_=bank[:].rearrange("p c k -> p (c k)"))
+            nc.scalar.copy(out=dst, in_=bank[:].rearrange("p c k -> p (c k)"))
 
-        def turn(src, out_views, sorted_words=None):
-            words = src.bitcast(F32)
-            for gp in range(2):
-                bank = psum.tile([P, 2, 2, P], F32, tag="fwd", bufs=4, name="fwd_bank")
-                for gi in range(2):
-                    g = 2 * gp + gi
-                    for u in range(2):
-                        if sorted_words is None:
-                            picked = words[:, 256 * g + u : 256 * (g + 1) : 2]
-                        else:
-                            picked = sorted_words[:, (2 * g + u) * P : (2 * g + u + 1) * P]
-                        nc.tensor.transpose(bank[:, gi, u, :], picked, ident[:])
-                nc.scalar.copy(out=out_views[gp], in_=bank[:].rearrange("p g u r -> p g r u"))
+        def fill_bank(sources):
+            bank = psum.tile([P, 2, 2, P], F32, tag="fwd", bufs=4, name="fwd_bank")
+            for j in range(2):
+                words = sources[j].bitcast(F32)
+                for u in range(2):
+                    nc.tensor.transpose(bank[:, j, u, :], words[:, u::2], ident[:])
+            return bank
 
-        sorted_of = {}
-
-        def sort_words(i):
-            if i >= n_tiles or i % 3 != 0:
-                return
-            sw = work.tile([P, 1024], F32, tag="sw", bufs=3, name="sw")
+        def turn_two(sources, out_words):
             nc.scalar.copy(
-                out=sw[:].rearrange("p (g u w) -> p g u w", g=PASSES, u=2),
-                in_=src_of[i][:].bitcast(F32).rearrange("p (g w u) -> p g u w", g=PASSES, u=2),
+                out=out_words.bitcast(F32).rearrange("p (j r u) -> p j r u", j=2, u=2),
+                in_=fill_bank(sources)[:].rearrange("p j u r -> p j r u"),
             )
-            sorted_of[i] = sw
 
         src_of = {}
         grp_of = {}
@@ -171,7 +160,7 @@ def tile_qwen2attention_pa_kernel(tc, x, Wq_bytes, Wq_scale, bq, Wkv, bkv, out_0
         uw_of = {}
 
         def product(i, part):
-            if i >= n_tiles:
+            if i >= n_tiles or on_scalar(i):
                 return
             kind, h = order[i]
             if kind == "q":
@@ -189,15 +178,52 @@ def tile_qwen2attention_pa_kernel(tc, x, Wq_bytes, Wq_scale, bq, Wkv, bkv, out_0
             else:
                 src_of[i] = wkv_raw[4 + h]
 
+        def on_scalar(i):
+            return i < n_tiles and i in (10, 19)
+
+        def widen(i, part):
+            if not on_scalar(i):
+                return
+            h = order[i][1]
+            if part == 0:
+                src_of[i] = work.tile([P, E], BF16, tag="wide", bufs=1, name="wide")
+            cols = slice(part * 1024, (part + 1) * 1024)
+            nc.scalar.copy(out=src_of[i][:, cols], in_=wq_bytes[h // 2][:, h % 2, cols].bitcast(FP8))
+
+        planes_of = {}
+
+        def turn_and_scale(i, gp):
+            if not on_scalar(i):
+                return
+            if gp == 0:
+                planes_of[i] = work.tile([P, PASSES, 4, P], BF16, tag="planes", bufs=1, name="planes")
+            bank = fill_bank([src_of[i][:, g * 512 : (g + 1) * 512] for g in (2 * gp, 2 * gp + 1)])
+            for j in range(2):
+                for u in range(2):
+                    pairs = bank[:, j, u, :].bitcast(BF16)
+                    for e in range(2):
+                        g, t = 2 * gp + j, 2 * u + e
+                        nc.scalar.activation(
+                            out=planes_of[i][:, g, t, :], in_=pairs[:, e::2], func=ACT.Copy, scale=scale_kp[:, g, t : t + 1]
+                        )
+
+        def interleave(i, gp):
+            if not on_scalar(i):
+                return
+            if gp == 0:
+                grp_of[i] = work.tile([P, E], BF16, tag="grp_late", bufs=1, align_bytes=64, name="grp_late")
+            nc.scalar.copy(
+                out=grp_of[i][:, gp * 1024 : (gp + 1) * 1024].rearrange("p (g r t) -> p g r t", g=2, t=4),
+                in_=planes_of[i][:, 2 * gp : 2 * gp + 2, :, :].rearrange("p g t r -> p g r t"),
+            )
+
         def turn_w(i):
-            if i >= n_tiles:
+            if i >= n_tiles or on_scalar(i):
                 return
             grp = work.tile([P, E], BF16, tag="grp", bufs=4, align_bytes=64, name="grp")
-            views = [
-                grp[:, gp * 1024 : (gp + 1) * 1024].bitcast(F32).rearrange("p (g r u) -> p g r u", g=2, u=2)
-                for gp in range(2)
-            ]
-            turn(src_of[i][:], views, sorted_of.get(i))
+            for gp in range(2):
+                sources = [src_of[i][:, g * 512 : (g + 1) * 512] for g in (2 * gp, 2 * gp + 1)]
+                turn_two(sources, grp[:, gp * 1024 : (gp + 1) * 1024])
             grp_of[i] = grp
 
         def quant(i):
@@ -235,13 +261,16 @@ def tile_qwen2attention_pa_kernel(tc, x, Wq_bytes, Wq_scale, bq, Wkv, bkv, out_0
         def pieces_of(i):
             return 2 if i == n_tiles - 1 else 1
 
+        def rope_after_turn(i):
+            return order[i][0] == "k"
+
         def rope(i):
             if i < 0 or i >= n_tiles:
                 return
             kind, h = order[i]
             acc = acc_of[i]
             uw = work.tile([P, 2, 512], F32, tag="uw", bufs=3, name="uw")
-            if kind == "v":
+            if kind == "v" or rope_after_turn(i):
                 nc.scalar.activation(out=uw[:, 0, :], in_=acc[:], func=ACT.Identity, bias=bias_col(i), scale=1.0)
             else:
                 width = 512 // pieces_of(i)
@@ -268,14 +297,15 @@ def tile_qwen2attention_pa_kernel(tc, x, Wq_bytes, Wq_scale, bq, Wkv, bkv, out_0
                 return
             kind, h = order[i]
             uw = uw_of[i]
-            o = work.tile([P, 512], F32, tag="o", bufs=3, name="o")
+            if not rope_after_turn(i):
+                o = work.tile([P, 512], F32, tag="o", bufs=3, name="o")
             blocks = TT // pieces_of(i)
             for piece in range(pieces_of(i)):
                 po = psum.tile([P, blocks, P], F32, tag="back", bufs=2, name="po")
                 for b in range(blocks):
                     tt = piece * blocks + b
                     cols = slice(tt * P, (tt + 1) * P)
-                    if kind == "v":
+                    if kind == "v" or rope_after_turn(i):
                         nc.tensor.transpose(po[:, b, :], uw[:, 0, cols], ident[:])
                     else:
                         nc.tensor.matmul(
@@ -285,51 +315,86 @@ def tile_qwen2attention_pa_kernel(tc, x, Wq_bytes, Wq_scale, bq, Wkv, bkv, out_0
                             out=po[:, b, :], lhsT=uw[:, 1, cols], rhs=swap[:], start=False, stop=True, is_transpose=True
                         )
                 part = slice(piece * blocks * P, (piece + 1) * blocks * P)
+                if rope_after_turn(i):
+                    turned_of[i] = po
+                    return
                 nc.scalar.copy(out=o[:, part], in_=po[:].rearrange("p t d -> p (t d)"))
                 nc.sync.dma_start(out=out_views[kind][h][:, part], in_=o[:, part])
 
-        x_grp = [const.tile([P, 2 * TT * P * 4], BF16, align_bytes=64, name="x_grp%d" % gp) for gp in range(2)]
+        turned_of = {}
+        terms_of = {}
 
-        def turn_x(tt):
-            views = [
-                x_grp[gp][:].bitcast(F32).rearrange("p (g t r u) -> p g t r u", g=2, t=TT, u=2)[:, :, tt, :, :]
-                for gp in range(2)
-            ]
-            turn(x_raw[tt][:], views)
+        def multiply_turned(i):
+            if i < 0 or i >= n_tiles or not rope_after_turn(i):
+                return
+            terms = work.tile([P, 2, 512], F32, tag="terms", bufs=2, name="terms")
+            nc.vector.tensor_tensor(
+                out=terms[:],
+                in0=turned_of[i][:].rearrange("p t d -> p (t d)").unsqueeze(1).to_broadcast([P, 2, 512]),
+                in1=cs_tok[:],
+                op=ALU.mult,
+            )
+            terms_of[i] = terms
+
+        def add_turned(i):
+            if i < 0 or i >= n_tiles or not rope_after_turn(i):
+                return
+            kind, h = order[i]
+            o = work.tile([P, 512], F32, tag="o", bufs=3, name="o")
+            halves = [terms_of[i][:, b, :].rearrange("p (t f d) -> p t f d", t=TT, f=2) for b in range(2)]
+            nc.vector.tensor_tensor(
+                out=o[:].rearrange("p (t f d) -> p t f d", t=TT, f=2),
+                in0=halves[0],
+                in1=halves[1][:, :, ::-1, :],
+                op=ALU.add,
+            )
+            nc.sync.dma_start(out=out_views[kind][h], in_=o[:])
+
+        x_grp = [const.tile([P, 2048], BF16, align_bytes=64, name="x_grp%d" % g) for g in range(PASSES)]
+        x_codes = []
+        x_scales = []
+
+        def turn_x(g):
+            for tp in range(2):
+                sources = [x_raw[g][:, 2 * tp + t, :] for t in range(2)]
+                turn_two(sources, x_grp[g][:, tp * 1024 : (tp + 1) * 1024])
+
+        def quant_x(g):
+            xc = const.tile([P, 512], U32, align_bytes=64, name="x_codes%d" % g)
+            xs = const.tile([P, 512], U8, align_bytes=64, name="x_scales%d" % g)
+            nc.vector.quantize_mx(out=xc[:].bitcast(FP8X4), scales=xs[:], in_=x_grp[g][:])
+            x_codes.append(xc)
+            x_scales.append(xs)
 
         for i in range(0, n_tiles, 3):
             product(i, 0)
         spread(0)
         spread(1)
+        turn_x(0)
         product(1, 0)
         spread(2)
         spread(3)
-        product(1, 1)
-        turn_x(0)
         turn_x(1)
-        product(2, 0)
-        product(2, 1)
-        turn_x(2)
-        turn_x(3)
+        product(1, 1)
+        quant_x(0)
         turn_w(0)
-        x_codes = []
-        x_scales = []
-        for g in range(PASSES):
-            xc = const.tile([P, 512], U32, align_bytes=64, name="x_codes%d" % g)
-            xs = const.tile([P, 512], U8, align_bytes=64, name="x_scales%d" % g)
-            nc.vector.quantize_mx(
-                out=xc[:].bitcast(FP8X4), scales=xs[:], in_=x_grp[g // 2][:, (g % 2) * 2048 : (g % 2 + 1) * 2048]
-            )
-            x_codes.append(xc)
-            x_scales.append(xs)
+        product(2, 0)
+        quant_x(1)
+        turn_x(2)
         quant(0)
+        turn_x(3)
+        quant_x(2)
+        quant_x(3)
         turn_w(1)
+        mx(0, 0, PASSES)
+        product(2, 1)
 
         y_sin = red_d[:].rearrange("p (t j) -> p t j", j=HALF)
         y_abs = const.tile([P, TT, HALF], F32, name="y_abs")
         nc.scalar.activation(out=y_abs[:], in_=y_sin, func=ACT.Abs)
-        cos_tok = const.tile([P, TT, P], F32, name="cos_tok")
-        sin_tok = const.tile([P, TT, P], F32, name="sin_tok")
+        cs_tok = const.tile([P, 2, TT * P], F32, name="cs_tok")
+        cos_tok = cs_tok[:, 0, :].rearrange("p (t d) -> p t d", d=P)
+        sin_tok = cs_tok[:, 1, :].rearrange("p (t d) -> p t d", d=P)
         nc.scalar.activation(out=sin_tok[:, :, 0:HALF], in_=y_sin, func=ACT.Sin)
         nc.scalar.activation(out=sin_tok[:, :, HALF:P], in_=y_sin, func=ACT.Sin, scale=-1.0)
         nc.scalar.activation(out=cos_tok[:, :, 0:HALF], in_=y_abs[:], func=ACT.Sin, scale=-1.0, bias=math.pi / 2.0)
@@ -346,7 +411,6 @@ def tile_qwen2attention_pa_kernel(tc, x, Wq_bytes, Wq_scale, bq, Wkv, bkv, out_0
         nc.scalar.copy(out=bias_ch[:], in_=bias_bank[:, 0:24])
 
         turn_w(2)
-        mx(0, 0, PASSES)
         quant(1)
         product(5, 0)
         product(5, 1)
@@ -363,7 +427,15 @@ def tile_qwen2attention_pa_kernel(tc, x, Wq_bytes, Wq_scale, bq, Wkv, bkv, out_0
             if step % 3 == 1:
                 product(step + 3, 1)
             back(step - 2)
+            multiply_turned(step - 2)
+            add_turned(step - 3)
             mx(step, 0, 2)
             turn_w(step + 2)
-            sort_words(step + 4)
+            turn_and_scale(step + 5, 0)
+            turn_and_scale(step + 4, 1)
+            interleave(step + 3, 0)
+            interleave(step + 2, 1)
+            widen(step + 7, 0)
+            widen(step + 6, 1)
             mx(step, 2, PASSES)
+        add_turned(n_tiles - 1)

@@ -31,11 +31,10 @@ PI_BELOW = 3.1415925
 def tile_qwen2attention_pa_kernel(tc, x, Wq_bytes, Wq_scale, bq, Wkv, bkv, out_0, out_1, out_2):
     nc = tc.nc
 
-    order = []
-    for i in range(8):
-        order.append(("v", i) if i < 4 else ("k", i - 4))
-        order.append(("q", 2 * i))
-        order.append(("q", 2 * i + 1))
+    order = [("v", 0), ("v", 1)]
+    for i, after in enumerate((("v", 2), ("v", 3), ("k", 0), ("k", 1), ("k", 2), ("k", 3))):
+        order += [("q", 2 * i), ("q", 2 * i + 1), after]
+    order += [("q", h) for h in range(12, 16)]
     n_tiles = len(order)
 
     with ExitStack() as ctx:
@@ -179,7 +178,7 @@ def tile_qwen2attention_pa_kernel(tc, x, Wq_bytes, Wq_scale, bq, Wkv, bkv, out_0
                 src_of[i] = wkv_raw[4 + h]
 
         def on_scalar(i):
-            return i < n_tiles and i in (10, 19)
+            return i < n_tiles and i in (12, 21)
 
         def widen(i, part):
             if not on_scalar(i):
@@ -262,7 +261,7 @@ def tile_qwen2attention_pa_kernel(tc, x, Wq_bytes, Wq_scale, bq, Wkv, bkv, out_0
             return 2 if i == n_tiles - 1 else 1
 
         def rope_after_turn(i):
-            return order[i][0] == "k"
+            return False
 
         def rope(i):
             if i < 0 or i >= n_tiles:
@@ -366,19 +365,20 @@ def tile_qwen2attention_pa_kernel(tc, x, Wq_bytes, Wq_scale, bq, Wkv, bkv, out_0
             x_codes.append(xc)
             x_scales.append(xs)
 
-        for i in range(0, n_tiles, 3):
-            product(i, 0)
+        for i in range(n_tiles):
+            if order[i][0] != "q":
+                product(i, 0)
         spread(0)
         spread(1)
         turn_x(0)
-        product(1, 0)
+        product(2, 0)
         spread(2)
         spread(3)
         turn_x(1)
-        product(1, 1)
+        product(2, 1)
         quant_x(0)
         turn_w(0)
-        product(2, 0)
+        product(3, 0)
         quant_x(1)
         turn_x(2)
         quant(0)
@@ -387,7 +387,7 @@ def tile_qwen2attention_pa_kernel(tc, x, Wq_bytes, Wq_scale, bq, Wkv, bkv, out_0
         quant_x(3)
         turn_w(1)
         mx(0, 0, PASSES)
-        product(2, 1)
+        product(3, 1)
 
         y_sin = red_d[:].rearrange("p (t j) -> p t j", j=HALF)
         y_abs = const.tile([P, TT, HALF], F32, name="y_abs")
@@ -399,6 +399,9 @@ def tile_qwen2attention_pa_kernel(tc, x, Wq_bytes, Wq_scale, bq, Wkv, bkv, out_0
         nc.scalar.activation(out=sin_tok[:, :, HALF:P], in_=y_sin, func=ACT.Sin, scale=-1.0)
         nc.scalar.activation(out=cos_tok[:, :, 0:HALF], in_=y_abs[:], func=ACT.Sin, scale=-1.0, bias=math.pi / 2.0)
         nc.scalar.activation(out=cos_tok[:, :, HALF:P], in_=y_abs[:], func=ACT.Sin, scale=-1.0, bias=math.pi / 2.0)
+        turn_w(2)
+        quant(1)
+
         cs_ch = const.tile([P, 2, 512], F32, name="cs_ch")
         for which, src_t in enumerate((cos_tok, sin_tok)):
             bank = psum.tile([P, TT, P], F32, tag="fwd", bufs=4, name="table_bank")
@@ -410,22 +413,15 @@ def tile_qwen2attention_pa_kernel(tc, x, Wq_bytes, Wq_scale, bq, Wkv, bkv, out_0
         bias_ch = const.tile([P, 24], F32, name="bias_ch")
         nc.scalar.copy(out=bias_ch[:], in_=bias_bank[:, 0:24])
 
-        turn_w(2)
-        quant(1)
-        product(5, 0)
-        product(5, 1)
+        halves = [(i, part) for i in range(3, n_tiles) for part in range(2) if order[i][0] == "q" and not on_scalar(i) and i > 4]
 
         for step in range(1, n_tiles + 2):
-            if step % 3 == 1:
-                product(step + 3, 0)
-            elif step % 3 == 2:
-                product(step + 6, 0)
-            else:
-                product(step + 5, 1)
+            if halves:
+                product(*halves.pop(0))
             rope(step - 1)
             quant(step + 1)
-            if step % 3 == 1:
-                product(step + 3, 1)
+            if halves and order[step - 1][0] == "v":
+                product(*halves.pop(0))
             back(step - 2)
             multiply_turned(step - 2)
             add_turned(step - 3)

from contextlib import ExitStack
import math

import concourse.mybir as mybir
from concourse.masks import make_identity

FLOPS = 2 * 512 * 2048 * 3072

F32 = mybir.dt.float32
BF16 = mybir.dt.bfloat16
I32 = mybir.dt.int32
U32 = mybir.dt.uint32
U8 = mybir.dt.uint8
FP8 = mybir.dt.float8_e4m3fn
FP8X4 = mybir.dt.float8_e4m3fn_x4
ALU = mybir.AluOpType
ACT = mybir.ActivationFunctionType

P = 128
E = 2048
PASSES = 4
TT = 4
HALF = 64
ROPE_THETA = 10000.0
TWO_PI = 2.0 * math.pi
TWO_PI_HEAD = 6.28125
TWO_PI_TAIL = TWO_PI - TWO_PI_HEAD
PI_BELOW = 3.1415925


def tile_qwen2attention_pa_kernel(tc, x, Wq_bytes, Wq_scale, bq, Wkv, bkv, out_0, out_1, out_2):
    nc = tc.nc

    order = [("v", 0), ("v", 1)]
    for i, after in enumerate((("v", 2), ("v", 3), ("k", 0), ("k", 1), ("k", 2), ("k", 3))):
        order += [("q", 2 * i), ("q", 2 * i + 1), after]
    order += [("q", h) for h in range(12, 16)]
    n_tiles = len(order)

    with ExitStack() as ctx:
        const = ctx.enter_context(tc.tile_pool(name="const", bufs=1))
        work = ctx.enter_context(tc.tile_pool(name="work", bufs=3))
        psum = ctx.enter_context(tc.psum_pool(name="psum", bufs=2))
        ctx.enter_context(tc.manual_schedule())

        scale_rows = const.tile([P, P], F32, name="scale_rows")
        nc.gpsimd.memset(scale_rows[:], 0.0)
        bias_rows = const.tile([P, P], BF16, name="bias_rows")
        nc.gpsimd.memset(bias_rows[:], 0.0)
        warm = const.tile([P, 2], F32, name="warm")
        nc.gpsimd.memset(warm[:, 0:1], 0.0)
        pos_i = const.tile([P, TT], I32, name="pos_i")
        nc.gpsimd.iota(pos_i[:], pattern=[[1, TT]], base=0, channel_multiplier=TT)
        ident = const.tile([P, P], F32, name="ident")
        make_identity(nc, ident[:])
        swap = const.tile([P, P], F32, name="swap")
        nc.gpsimd.tensor_copy(out=swap[:, 0:HALF], in_=ident[:, HALF:P])
        nc.gpsimd.tensor_copy(out=swap[:, HALF:P], in_=ident[:, 0:HALF])

        nc.sync.dma_start(out=scale_rows[0:16, :], in_=Wq_scale.rearrange("o (c p) -> (o c) p", p=P))
        nc.sync.dma_start(out=bias_rows[0:16, :], in_=bq.rearrange("(c p) -> c p", p=P))
        nc.sync.dma_start(out=bias_rows[16:24, :], in_=bkv.rearrange("(c p) -> c p", p=P))
        bias_f32 = const.tile([P, P], F32, name="bias_f32")
        nc.gpsimd.tensor_copy(out=bias_f32[:], in_=bias_rows[:])

        wq_view = Wq_bytes.rearrange("(m p) k -> p m k", p=P)
        wq_bytes = {}
        wkv_raw = {}
        x_raw = []

        def load_wq(pair):
            t = const.tile([P, 2, E], U8, name="wq_bytes%d" % pair)
            nc.sync.dma_start(out=t[:], in_=wq_view[:, 2 * pair : 2 * pair + 2, :])
            wq_bytes[pair] = t

        def load_wkv(m):
            t = const.tile([P, E], BF16, name="wkv_raw%d" % m)
            nc.sync.dma_start(out=t[:], in_=Wkv[m * P : (m + 1) * P, :])
            wkv_raw[m] = t

        load_wq(0)
        scale_kp = const.tile([P, PASSES, 4], F32, name="scale_kp")
        x_view = x.rearrange("o (p t) k -> p (o t) k", t=TT)
        for g in range(PASSES):
            t = const.tile([P, TT, 512], BF16, name="x_raw%d" % g)
            nc.sync.dma_start(out=t[:], in_=x_view[:, :, g * 512 : (g + 1) * 512])
            x_raw.append(t)
            if g == 1:
                load_wkv(4)
        nc.sync.dma_start(out=scale_kp[:], in_=Wq_scale.rearrange("o (g p t) -> p (o g) t", p=P, t=4))
        for kind, h in order[1:]:
            if kind == "q":
                if h // 2 not in wq_bytes:
                    load_wq(h // 2)
            else:
                load_wkv(h if kind == "k" else 4 + h)

        nc.scalar.activation(out=warm[:, 1:2], in_=warm[:, 0:1], func=ACT.Sin)
        pos = const.tile([P, TT], F32, name="pos")
        nc.vector.tensor_copy(out=pos[:], in_=pos_i[:])
        freq = const.tile([P, HALF], F32, name="freq")
        nc.vector.memset(freq[:, 0:1], 1.0)
        for b in range(6):
            n = 1 << b
            nc.vector.tensor_scalar(
                out=freq[:, n : 2 * n], in0=freq[:, 0:n], scalar1=ROPE_THETA ** (-n / 64.0), scalar2=None, op0=ALU.mult
            )
        ang = const.tile([P, TT * HALF], F32, name="ang")
        for tt in range(TT):
            nc.vector.tensor_scalar(
                out=ang[:, tt * HALF : (tt + 1) * HALF], in0=freq[:], scalar1=pos[:, tt : tt + 1], scalar2=None, op0=ALU.mult
            )
        turns_i = const.tile([P, 256], I32, name="turns_i")
        nc.vector.tensor_scalar(out=turns_i[:], in0=ang[:], scalar1=1.0 / TWO_PI, scalar2=None, op0=ALU.mult)
        turns = const.tile([P, 256], F32, name="turns")
        nc.vector.tensor_copy(out=turns[:], in_=turns_i[:])
        red_a = const.tile([P, 256], F32, name="red_a")
        nc.vector.scalar_tensor_tensor(out=red_a[:], in0=turns[:], scalar=-TWO_PI_HEAD, in1=ang[:], op0=ALU.mult, op1=ALU.add)
        red_b = const.tile([P, 256], F32, name="red_b")
        nc.vector.scalar_tensor_tensor(out=red_b[:], in0=turns[:], scalar=-TWO_PI_TAIL, in1=red_a[:], op0=ALU.mult, op1=ALU.add)
        wrap = const.tile([P, 256], F32, name="wrap")
        nc.vector.tensor_scalar(out=wrap[:], in0=red_b[:], scalar1=math.pi, scalar2=-TWO_PI, op0=ALU.is_gt, op1=ALU.mult)
        red_c = const.tile([P, 256], F32, name="red_c")
        nc.vector.tensor_tensor(out=red_c[:], in0=red_b[:], in1=wrap[:], op=ALU.add)
        red_d = const.tile([P, 256], F32, name="red_d")
        nc.vector.tensor_scalar(out=red_d[:], in0=red_c[:], scalar1=PI_BELOW, scalar2=-PI_BELOW, op0=ALU.min, op1=ALU.max)

        scale_bank = psum.tile([P, P], F32, tag="fwd", bufs=4, name="scale_bank")
        nc.tensor.transpose(scale_bank[:], scale_rows[:], ident[:])
        scale_col = const.tile([P, 16], F32, name="scale_col")
        nc.scalar.copy(out=scale_col[:], in_=scale_bank[:, 0:16])
        scale_all = [const.tile([P, 1024], F32, name="scale_all%d" % part) for part in range(2)]

        def spread(b):
            bank = psum.tile([P, 4, P], F32, tag="fwd", bufs=4, name="spread_bank")
            for c in range(4):
                nc.tensor.transpose(bank[:, c, :], scale_col[:, 4 * b + c : 4 * b + c + 1].to_broadcast([P, P]), ident[:])
            dst = scale_all[b // 2][:, (b % 2) * 512 : (b % 2 + 1) * 512]
            nc.scalar.copy(out=dst, in_=bank[:].rearrange("p c k -> p (c k)"))

        def fill_bank(sources):
            bank = psum.tile([P, 2, 2, P], F32, tag="fwd", bufs=4, name="fwd_bank")
            for j in range(2):
                words = sources[j].bitcast(F32)
                for u in range(2):
                    nc.tensor.transpose(bank[:, j, u, :], words[:, u::2], ident[:])
            return bank

        def turn_two(sources, out_words):
            nc.scalar.copy(
                out=out_words.bitcast(F32).rearrange("p (j r u) -> p j r u", j=2, u=2),
                in_=fill_bank(sources)[:].rearrange("p j u r -> p j r u"),
            )

        src_of = {}
        grp_of = {}
        codes_of = {}
        acc_of = {}
        uw_of = {}

        def product(i, part):
            if i >= n_tiles or on_scalar(i):
                return
            kind, h = order[i]
            if kind == "q":
                if part == 0:
                    src_of[i] = work.tile([P, E], BF16, tag="wbf", bufs=6, name="wbf")
                cols = slice(part * 1024, (part + 1) * 1024)
                nc.vector.tensor_tensor(
                    out=src_of[i][:, cols],
                    in0=wq_bytes[h // 2][:, h % 2, cols].bitcast(FP8),
                    in1=scale_all[part][:],
                    op=ALU.mult,
                )
            elif kind == "k":
                src_of[i] = wkv_raw[h]
            else:
                src_of[i] = wkv_raw[4 + h]

        def on_scalar(i):
            return i < n_tiles and i in (12, 21)

        def widen(i, part):
            if not on_scalar(i):
                return
            h = order[i][1]
            if part == 0:
                src_of[i] = work.tile([P, E], BF16, tag="wide", bufs=1, name="wide")
            cols = slice(part * 1024, (part + 1) * 1024)
            nc.scalar.copy(out=src_of[i][:, cols], in_=wq_bytes[h // 2][:, h % 2, cols].bitcast(FP8))

        planes_of = {}

        def turn_and_scale(i, gp):
            if not on_scalar(i):
                return
            if gp == 0:
                planes_of[i] = work.tile([P, PASSES, 4, P], BF16, tag="planes", bufs=1, name="planes")
            bank = fill_bank([src_of[i][:, g * 512 : (g + 1) * 512] for g in (2 * gp, 2 * gp + 1)])
            for j in range(2):
                for u in range(2):
                    pairs = bank[:, j, u, :].bitcast(BF16)
                    for e in range(2):
                        g, t = 2 * gp + j, 2 * u + e
                        nc.scalar.activation(
                            out=planes_of[i][:, g, t, :], in_=pairs[:, e::2], func=ACT.Copy, scale=scale_kp[:, g, t : t + 1]
                        )

        def interleave(i, gp):
            if not on_scalar(i):
                return
            if gp == 0:
                grp_of[i] = work.tile([P, E], BF16, tag="grp_late", bufs=1, align_bytes=64, name="grp_late")
            nc.scalar.copy(
                out=grp_of[i][:, gp * 1024 : (gp + 1) * 1024].rearrange("p (g r t) -> p g r t", g=2, t=4),
                in_=planes_of[i][:, 2 * gp : 2 * gp + 2, :, :].rearrange("p g t r -> p g r t"),
            )

        def turn_w(i):
            if i >= n_tiles or on_scalar(i):
                return
            grp = work.tile([P, E], BF16, tag="grp", bufs=4, align_bytes=64, name="grp")
            for gp in range(2):
                sources = [src_of[i][:, g * 512 : (g + 1) * 512] for g in (2 * gp, 2 * gp + 1)]
                turn_two(sources, grp[:, gp * 1024 : (gp + 1) * 1024])
            grp_of[i] = grp

        def quant(i):
            if i >= n_tiles:
                return
            wc = work.tile([P, 512], U32, tag="wc", bufs=3, align_bytes=64, name="wc")
            ws = work.tile([P, 512], U8, tag="ws", bufs=3, align_bytes=64, name="ws")
            nc.vector.quantize_mx(out=wc[:].bitcast(FP8X4), scales=ws[:], in_=grp_of[i][:])
            codes_of[i] = (wc, ws)

        def mx(i, first, last):
            if i >= n_tiles:
                return
            wc, ws = codes_of[i]
            if first == 0:
                acc_of[i] = psum.tile([P, 512], F32, tag="acc", bufs=2, name="acc")
            acc = acc_of[i]
            for g in range(first, last):
                cols = slice(g * P, (g + 1) * P)
                nc.tensor.matmul_mx(
                    out=acc[:],
                    lhsT=wc[:, cols].bitcast(FP8X4),
                    lhsT_scale=ws[:, cols],
                    rhs=x_codes[g][:].bitcast(FP8X4),
                    rhs_scale=x_scales[g][:],
                    start=(g == 0),
                    stop=(g == PASSES - 1),
                )

        def bias_col(i):
            kind, h = order[i]
            m = h if kind == "q" else (16 + h if kind == "k" else 20 + h)
            return bias_ch[:, m : m + 1]

        def pieces_of(i):
            return 2 if i == n_tiles - 1 else 1

        def rope_after_turn(i):
            return False

        def rope(i):
            if i < 0 or i >= n_tiles:
                return
            kind, h = order[i]
            acc = acc_of[i]
            uw = work.tile([P, 2, 512], F32, tag="uw", bufs=3, name="uw")
            if kind == "v" or rope_after_turn(i):
                nc.scalar.activation(out=uw[:, 0, :], in_=acc[:], func=ACT.Identity, bias=bias_col(i), scale=1.0)
            else:
                width = 512 // pieces_of(i)
                for piece in range(pieces_of(i)):
                    cols = slice(piece * width, (piece + 1) * width)
                    nc.vector.scalar_tensor_tensor(
                        out=uw[:, :, cols],
                        in0=acc[:, cols].unsqueeze(1).to_broadcast([P, 2, width]),
                        scalar=bias_col(i),
                        in1=cs_ch[:, :, cols],
                        op0=ALU.add,
                        op1=ALU.mult,
                    )
            uw_of[i] = uw

        out_views = {
            "q": out_0.rearrange("o h (p t) d -> (o h) p (t d)", t=TT),
            "k": out_1.rearrange("o h (p t) d -> (o h) p (t d)", t=TT),
            "v": out_2.rearrange("o h (p t) d -> (o h) p (t d)", t=TT),
        }

        def back(i):
            if i < 0 or i >= n_tiles:
                return
            kind, h = order[i]
            uw = uw_of[i]
            if not rope_after_turn(i):
                o = work.tile([P, 512], F32, tag="o", bufs=3, name="o")
            blocks = TT // pieces_of(i)
            for piece in range(pieces_of(i)):
                po = psum.tile([P, blocks, P], F32, tag="back", bufs=2, name="po")
                for b in range(blocks):
                    tt = piece * blocks + b
                    cols = slice(tt * P, (tt + 1) * P)
                    if kind == "v" or rope_after_turn(i):
                        nc.tensor.transpose(po[:, b, :], uw[:, 0, cols], ident[:])
                    else:
                        nc.tensor.matmul(
                            out=po[:, b, :], lhsT=uw[:, 0, cols], rhs=ident[:], start=True, stop=False, is_transpose=True
                        )
                        nc.tensor.matmul(
                            out=po[:, b, :], lhsT=uw[:, 1, cols], rhs=swap[:], start=False, stop=True, is_transpose=True
                        )
                part = slice(piece * blocks * P, (piece + 1) * blocks * P)
                if rope_after_turn(i):
                    turned_of[i] = po
                    return
                nc.scalar.copy(out=o[:, part], in_=po[:].rearrange("p t d -> p (t d)"))
                nc.sync.dma_start(out=out_views[kind][h][:, part], in_=o[:, part])

        turned_of = {}
        terms_of = {}

        def multiply_turned(i):
            if i < 0 or i >= n_tiles or not rope_after_turn(i):
                return
            terms = work.tile([P, 2, 512], F32, tag="terms", bufs=2, name="terms")
            nc.vector.tensor_tensor(
                out=terms[:],
                in0=turned_of[i][:].rearrange("p t d -> p (t d)").unsqueeze(1).to_broadcast([P, 2, 512]),
                in1=cs_tok[:],
                op=ALU.mult,
            )
            terms_of[i] = terms

        def add_turned(i):
            if i < 0 or i >= n_tiles or not rope_after_turn(i):
                return
            kind, h = order[i]
            o = work.tile([P, 512], F32, tag="o", bufs=3, name="o")
            halves = [terms_of[i][:, b, :].rearrange("p (t f d) -> p t f d", t=TT, f=2) for b in range(2)]
            nc.vector.tensor_tensor(
                out=o[:].rearrange("p (t f d) -> p t f d", t=TT, f=2),
                in0=halves[0],
                in1=halves[1][:, :, ::-1, :],
                op=ALU.add,
            )
            nc.sync.dma_start(out=out_views[kind][h], in_=o[:])

        x_grp = [const.tile([P, 2048], BF16, align_bytes=64, name="x_grp%d" % g) for g in range(PASSES)]
        x_codes = []
        x_scales = []

        def turn_x(g):
            for tp in range(2):
                sources = [x_raw[g][:, 2 * tp + t, :] for t in range(2)]
                turn_two(sources, x_grp[g][:, tp * 1024 : (tp + 1) * 1024])

        def quant_x(g):
            xc = const.tile([P, 512], U32, align_bytes=64, name="x_codes%d" % g)
            xs = const.tile([P, 512], U8, align_bytes=64, name="x_scales%d" % g)
            nc.vector.quantize_mx(out=xc[:].bitcast(FP8X4), scales=xs[:], in_=x_grp[g][:])
            x_codes.append(xc)
            x_scales.append(xs)

        for i in range(n_tiles):
            if order[i][0] != "q":
                product(i, 0)
        spread(0)
        spread(1)
        turn_x(0)
        product(2, 0)
        spread(2)
        spread(3)
        turn_x(1)
        product(2, 1)
        quant_x(0)
        turn_w(0)
        product(3, 0)
        quant_x(1)
        turn_x(2)
        quant(0)
        turn_x(3)
        quant_x(2)
        quant_x(3)
        turn_w(1)
        mx(0, 0, PASSES)
        product(3, 1)

        y_sin = red_d[:].rearrange("p (t j) -> p t j", j=HALF)
        y_abs = const.tile([P, TT, HALF], F32, name="y_abs")
        nc.scalar.activation(out=y_abs[:], in_=y_sin, func=ACT.Abs)
        cs_tok = const.tile([P, 2, TT * P], F32, name="cs_tok")
        cos_tok = cs_tok[:, 0, :].rearrange("p (t d) -> p t d", d=P)
        sin_tok = cs_tok[:, 1, :].rearrange("p (t d) -> p t d", d=P)
        nc.scalar.activation(out=sin_tok[:, :, 0:HALF], in_=y_sin, func=ACT.Sin)
        nc.scalar.activation(out=sin_tok[:, :, HALF:P], in_=y_sin, func=ACT.Sin, scale=-1.0)
        nc.scalar.activation(out=cos_tok[:, :, 0:HALF], in_=y_abs[:], func=ACT.Sin, scale=-1.0, bias=math.pi / 2.0)
        nc.scalar.activation(out=cos_tok[:, :, HALF:P], in_=y_abs[:], func=ACT.Sin, scale=-1.0, bias=math.pi / 2.0)
        turn_w(2)
        quant(1)

        cs_ch = const.tile([P, 2, 512], F32, name="cs_ch")
        for which, src_t in enumerate((cos_tok, sin_tok)):
            bank = psum.tile([P, TT, P], F32, tag="fwd", bufs=4, name="table_bank")
            for tt in range(TT):
                nc.tensor.transpose(bank[:, tt, :], src_t[:, tt, :], ident[:])
            nc.scalar.copy(out=cs_ch[:, which, :], in_=bank[:].rearrange("p t s -> p (t s)"))
        bias_bank = psum.tile([P, P], F32, tag="fwd", bufs=4, name="bias_bank")
        nc.tensor.transpose(bias_bank[:], bias_f32[:], ident[:])
        bias_ch = const.tile([P, 24], F32, name="bias_ch")
        nc.scalar.copy(out=bias_ch[:], in_=bias_bank[:, 0:24])

        halves = [(i, part) for i in range(3, n_tiles) for part in range(2) if order[i][0] == "q" and not on_scalar(i) and i > 4]

        for step in range(1, n_tiles + 2):
            if halves:
                product(*halves.pop(0))
            rope(step - 1)
            quant(step + 1)
            if halves and order[step - 1][0] == "v":
                product(*halves.pop(0))
            back(step - 2)
            multiply_turned(step - 2)
            add_turned(step - 3)
            mx(step, 0, 2)
            turn_w(step + 2)
            turn_and_scale(step + 5, 0)
            turn_and_scale(step + 4, 1)
            interleave(step + 3, 0)
            interleave(step + 2, 1)
            widen(step + 7, 0)
            widen(step + 6, 1)
            mx(step, 2, PASSES)
        add_turned(n_tiles - 1)
